import numpy as np
import ml_dtypes


def mxq(x, axis, fmt="e4m3"):
    dtype, down = {"e4m3": (ml_dtypes.float8_e4m3fn, 7), "e5m2": (ml_dtypes.float8_e5m2, 14)}[fmt]
    v = np.moveaxis(np.asarray(x, np.float32).astype(ml_dtypes.bfloat16).astype(np.float64), axis, -1)
    blocks = v.reshape(v.shape[:-1] + (-1, 32))
    amax = np.abs(blocks).max(-1, keepdims=True)
    byte = np.maximum(np.where(amax > 0, np.frexp(amax)[1] - 1 + 127, 0) - down, 1)
    scale = np.exp2(byte - 127.0)
    codes = (blocks / scale).astype(np.float32).astype(dtype).astype(np.float64)
    return np.moveaxis((codes * scale).reshape(v.shape), -1, axis)


WIDE = False


def mx_kscale(k):
    if not WIDE:
        return np.ones(k)
    levels = np.array([10, -10, 5, -5, 0])
    a = np.random.permutation(np.resize(levels, k // 512 * 4)).reshape(k // 512, 4)
    idx = np.arange(k)
    return np.exp2(a[idx // 512, idx % 128 // 32])


BF16 = ml_dtypes.bfloat16


def bf(x):
    return np.asarray(x, np.float32).astype(BF16)


def f64(x):
    return np.asarray(x).astype(np.float64)


B, S, H, I = 8, 512, 512, 512


def silu(v):
    return v / (1.0 + np.exp(-v))


def setup_inputs():
    s = mx_kscale(H)
    c = np.exp2(-np.round(0.25 * np.log2(np.mean(1.0 / s**2))))
    t = c * np.exp2(np.round(np.log2(mx_kscale(I)) / 2))
    return {"hidden_state": bf(np.random.standard_normal((B, S, H)) * s),
            "w_gate": bf(np.random.standard_normal((I, H)) * 1.0 / np.sqrt(H) / s[None, :]),
            "w_up": bf(np.random.standard_normal((I, H)) * 0.8 / np.sqrt(H) / s[None, :] * t[:, None]),
            "w_down": bf(np.random.standard_normal((H, I)) * 2.0 / np.sqrt(I) / t[None, :])}


def reference(hidden_state, w_gate, w_up, w_down):
    xq = mxq(f64(hidden_state), 2, "e4m3")
    wu = f64(w_up)
    gate = silu(xq @ mxq(f64(w_gate), 1, "e4m3").T)
    up = xq @ mxq(wu, 1, "e4m3").T
    intermediate = gate * up
    s = np.sum(intermediate ** 2, axis=1)
    row_sq = np.sum(wu ** 2, axis=-1)
    impacts = np.sqrt(s * row_sq[None, :])
    out = mxq(intermediate, 2, "e4m3") @ mxq(f64(w_down), 1, "e4m3").T
    return out, impacts

@@ -1,0 +1,275 @@
+from contextlib import ExitStack
+
+import concourse.mybir as mybir
+from concourse.masks import make_identity
+
+F32 = mybir.dt.float32
+BF16 = mybir.dt.bfloat16
+U32 = mybir.dt.uint32
+U8 = mybir.dt.uint8
+FP8X4 = mybir.dt.float8_e4m3fn_x4
+ACT = mybir.ActivationFunctionType
+ALU = mybir.AluOpType
+
+P = 128
+NB = 8
+S = 512
+H = 512
+I = 512
+NT = 4
+FLOPS = 3 * 2 * NB * S * H * I
+
+PINNED = True
+GP_CAST = True
+
+
+def tile_qwen2mlp_nd_t_kernel(tc, hidden_state, w_gate, w_up, w_down, out_0, out_1):
+    nc = tc.nc
+    with ExitStack() as ctx:
+        const = ctx.enter_context(tc.tile_pool(name="const", bufs=1))
+        xin = ctx.enter_context(tc.tile_pool(name="xin", bufs=NB))
+        work = ctx.enter_context(tc.tile_pool(name="work", bufs=2))
+        psum = ctx.enter_context(tc.psum_pool(name="psum", bufs=2))
+        if PINNED:
+            ctx.enter_context(tc.manual_schedule())
+
+        x_view = hidden_state.rearrange("b (p j) h -> b p j h", j=NT)
+        o_view = out_0.rearrange("b (p j) n -> b p j n", j=NT)
+        x_sb = {}
+        w_sb = {}
+
+        def load_x(b):
+            x_raw = xin.tile([P, NT * H], BF16, name="x_raw")
+            nc.sync.dma_start(out=x_raw[:].rearrange("p (j h) -> p j h", j=NT), in_=x_view[b])
+            x_sb[b] = x_raw
+
+        def load_w(key, view):
+            w_raw = const.tile([P, NT * H], BF16, name="w_raw_" + key)
+            nc.sync.dma_start(out=w_raw[:].rearrange("p (r k) -> p r k", r=NT), in_=view)
+            w_sb[key] = w_raw
+
+        load_x(0)
+        load_w("g", w_gate.rearrange("(p t) k -> p t k", t=NT))
+        load_w("u", w_up.rearrange("(p t) k -> p t k", t=NT))
+        load_x(1)
+        load_w("d", w_down.rearrange("(r p) k -> p r k", p=P))
+        for b in range(2, NB):
+            load_x(b)
+
+        warm = const.tile([P, 2], F32, name="warm")
+        nc.vector.memset(warm[:, 0:1], 0.0)
+        nc.scalar.activation(out=warm[:, 1:2], in_=warm[:, 0:1], func=ACT.Silu)
+
+        ident = const.tile([P, P], F32, name="ident")
+        make_identity(nc, ident[:])
+        imp_pad = const.tile([P, NT, P], F32, name="imp_pad")
+        nc.gpsimd.memset(imp_pad[:], 0.0)
+        ssum = const.tile([P, NT, NB], F32, name="ssum")
+        row_sq = const.tile([P, NT], F32, name="row_sq")
+
+        banks = {}
+        grouped = {}
+        codes = {}
+        planes = {}
+
+        def transposes(key, raw, pairs_apart):
+            words = raw[:].bitcast(F32)
+            if pairs_apart:
+                view = words.rearrange("p (r q u) -> p r u q", r=NT, u=2)
+            else:
+                view = words.rearrange("p (r u q) -> p r u q", r=NT, u=2)
+            for c in range(2):
+                bank = psum.tile([P, 2, 2 * P], F32, name="xt", tag="xt")
+                for rr in range(2):
+                    for u in range(2):
+                        nc.tensor.transpose(bank[:, u, rr * P:(rr + 1) * P], view[:, 2 * c + rr, u, :], ident[:])
+                banks[(key, c)] = bank
+
+        def evacuate(key, c, on_scalar):
+            if c == 0:
+                grp = work.tile([P, 4 * S], BF16, name="grp", tag="grp", align_bytes=64)
+                grouped[key] = grp
+            dst = grouped[key][:].bitcast(F32).rearrange("p (s u) -> p s u", u=2)[:, c * 2 * P:(c + 1) * 2 * P, :]
+            src = banks[(key, c)][:].rearrange("p u s -> p s u")
+            if on_scalar:
+                nc.scalar.copy(out=dst, in_=src)
+            else:
+                nc.vector.tensor_copy(out=dst, in_=src)
+
+        def quantise(key, pool, bufs, tag):
+            cod = pool.tile([P, S], U32, name="cod_" + tag, tag="cod_" + tag, bufs=bufs, align_bytes=64)
+            pla = pool.tile([P, S], U8, name="pla_" + tag, tag="pla_" + tag, bufs=bufs, align_bytes=64)
+            nc.vector.quantize_mx(out=cod[:].bitcast(FP8X4), scales=pla[:], in_=grouped[key][:])
+            codes[key] = cod
+            planes[key] = pla
+
+        def ok(b):
+            return 0 <= b < NB
+
+        acc = {}
+        sg = {}
+        hf = {}
+
+        def pass1(b, t, which):
+            if not ok(b):
+                return
+            bank = psum.tile([P, S], F32, name="ps_" + which, tag="ps_" + which)
+            cols = slice(t * P, (t + 1) * P)
+            nc.tensor.matmul_mx(
+                out=bank[:],
+                lhsT=codes[which][:, cols].bitcast(FP8X4), lhsT_scale=planes[which][:, cols],
+                rhs=codes[b][:].bitcast(FP8X4), rhs_scale=planes[b][:],
+                start=True, stop=True)
+            acc[(which, b, t)] = bank
+
+        def silu(b, t):
+            if not ok(b):
+                return
+            s_g = work.tile([P, S], F32, name="s_g", tag="s_g", bufs=4)
+            nc.scalar.activation(out=s_g[:], in_=acc[("g", b, t)][:], func=ACT.Silu)
+            sg[(b, t)] = s_g
+
+        def mult(b, t):
+            if not ok(b):
+                return
+            if t == 0:
+                h_f = work.tile([P, NT, S], F32, name="h_f", tag="h_f", bufs=2)
+                hf[b] = h_f
+            nc.vector.tensor_tensor(out=hf[b][:, t, :], in0=sg[(b, t)][:], in1=acc[("u", b, t)][:], op=ALU.mult)
+
+        def square(b, t):
+            if not ok(b):
+                return
+            junk = work.tile([P, S], BF16, name="junk", tag="junk")
+            nc.scalar.activation(out=junk[:], in_=hf[b][:, t, :], func=ACT.Square, accum_out=ssum[:, t, b:b + 1])
+
+        def cast(b):
+            if not ok(b):
+                return
+            grp = work.tile([P, 4 * S], BF16, name="hgrp", tag="hgrp", align_bytes=64)
+            grouped[("h", b)] = grp
+            dst = grp[:].rearrange("p (s t) -> p s t", t=NT)
+            src = hf[b][:].rearrange("p t s -> p s t")
+            if GP_CAST and b < NB - 1:
+                nc.gpsimd.tensor_scalar(out=dst, in0=src, scalar1=1.0, scalar2=0.0, op0=ALU.mult, op1=ALU.add)
+            else:
+                nc.vector.tensor_copy(out=dst, in_=src)
+
+        def quant_h(b):
+            if ok(b):
+                quantise(("h", b), work, 2, "h")
+
+        ob = {}
+
+        def pass2(b, j):
+            if not ok(b):
+                return
+            bank = psum.tile([P, H], F32, name="ps_o", tag="ps_o")
+            cols = slice(j * P, (j + 1) * P)
+            nc.tensor.matmul_mx(
+                out=bank[:],
+                lhsT=codes[("h", b)][:, cols].bitcast(FP8X4), lhsT_scale=planes[("h", b)][:, cols],
+                rhs=codes["d"][:].bitcast(FP8X4), rhs_scale=planes["d"][:],
+                start=True, stop=True)
+            acc[("o", b, j)] = bank
+
+        def evac_o(b, j):
+            if not ok(b):
+                return
+            if j == 0:
+                o_sb = work.tile([P, NT, H], F32, name="o_sb", tag="o_sb", bufs=3)
+                ob[b] = o_sb
+            if b == NB - 1 and j % 2 == 1:
+                nc.scalar.copy(out=ob[b][:, j, :], in_=acc[("o", b, j)][:])
+            else:
+                nc.vector.tensor_copy(out=ob[b][:, j, :], in_=acc[("o", b, j)][:])
+
+        def store(b, j0, j1):
+            if ok(b):
+                nc.sync.dma_start(out=o_view[b][:, j0:j1, :], in_=ob[b][:, j0:j1, :])
+
+        def prep_x_t(b):
+            if ok(b):
+                transposes(b, x_sb[b], False)
+
+        def prep_x_e(b):
+            if ok(b):
+                evacuate(b, 0, True)
+                evacuate(b, 1, True)
+
+        def prep_x_q(b):
+            if ok(b):
+                quantise(b, work, 3, "x")
+
+        def head_group(key, raw, pairs_apart, is_weight):
+            transposes(key, raw, pairs_apart)
+            evacuate(key, 0, True)
+            evacuate(key, 1, False)
+            if is_weight:
+                quantise(key, const, 1, "w" + key)
+            else:
+                quantise(key, work, 3, "x")
+
+        head_group(0, x_sb[0], False, False)
+        head_group("g", w_sb["g"], False, True)
+        head_group("u", w_sb["u"], False, True)
+        for t in range(2):
+            pass1(0, t, "g")
+            pass1(0, t, "u")
+        wu3 = w_sb["u"][:].rearrange("p (t k) -> p t k", t=NT)
+        for t in range(NT):
+            junk = work.tile([P, S], BF16, name="junk", tag="junk")
+            nc.scalar.activation(out=junk[:], in_=wu3[:, t, :], func=ACT.Square, accum_out=row_sq[:, t:t + 1])
+        head_group(1, x_sb[1], False, False)
+        head_group("d", w_sb["d"], True, True)
+        prep_x_t(2)
+
+        for i in range(NB + 1):
+            silu(i, 0)
+            pass1(i, 2, "g")
+            mult(i, 0)
+            silu(i, 1)
+            pass1(i, 2, "u")
+            pass1(i, 3, "g")
+            mult(i, 1)
+            pass1(i, 3, "u")
+            silu(i, 2)
+            quant_h(i - 1)
+            silu(i, 3)
+            pass2(i - 1, 0)
+            pass2(i - 1, 1)
+            mult(i, 2)
+            pass1(i + 1, 0, "g")
+            pass1(i + 1, 0, "u")
+            mult(i, 3)
+            cast(i)
+            pass1(i + 1, 1, "g")
+            pass1(i + 1, 1, "u")
+            prep_x_e(i + 2)
+            evac_o(i - 1, 0)
+            evac_o(i - 1, 1)
+            if i == NB:
+                store(i - 1, 0, 2)
+            pass2(i - 1, 2)
+            pass2(i - 1, 3)
+            evac_o(i - 1, 2)
+            evac_o(i - 1, 3)
+            if i == NB:
+                store(i - 1, 2, 4)
+            else:
+                store(i - 1, 0, 4)
+            prep_x_t(i + 3)
+            for t in range(NT):
+                square(i, t)
+            if i == NB - 1:
+                for t in range(NT):
+                    nc.scalar.activation(out=imp_pad[:, t, 0:NB], in_=ssum[:, t, :], func=ACT.Sqrt,
+                                         scale=row_sq[:, t:t + 1])
+            prep_x_q(i + 2)
+
+        imp_t = psum.tile([P, NT, P], F32, name="imp_t", tag="xt")
+        for t in range(NT):
+            nc.tensor.transpose(imp_t[:, t, :], imp_pad[:, t, :], ident[:])
+        imp_sb = const.tile([P, P, NT], F32, name="imp_sb")
+        nc.scalar.copy(out=imp_sb[:], in_=imp_t[:].rearrange("c t p -> c p t"))
+        nc.sync.dma_start(out=out_1, in_=imp_sb[0:NB].rearrange("c p t -> c (p t)"))

@@ -52,8 +52,9 @@ def tile_qwen2mlp_nd_t_kernel(tc, hidden_state, w_gate, w_up, w_down, out_0, out
         load_w("g", w_gate.rearrange("(p t) k -> p t k", t=NT))
         load_w("u", w_up.rearrange("(p t) k -> p t k", t=NT))
         load_x(1)
+        load_x(2)
         load_w("d", w_down.rearrange("(r p) k -> p r k", p=P))
-        for b in range(2, NB):
+        for b in range(3, NB):
             load_x(b)
 
         warm = const.tile([P, 2], F32, name="warm")
@@ -64,7 +65,9 @@ def tile_qwen2mlp_nd_t_kernel(tc, hidden_state, w_gate, w_up, w_down, out_0, out
         make_identity(nc, ident[:])
         imp_pad = const.tile([P, NT, P], F32, name="imp_pad")
         nc.gpsimd.memset(imp_pad[:], 0.0)
-        ssum = const.tile([P, NT, NB], F32, name="ssum")
+        half = const.tile([P, NT], F32, name="half")
+        nc.gpsimd.memset(half[:], 0.5)
+        ssum = const.tile([P, NB, NT], F32, name="ssum")
         row_sq = const.tile([P, NT], F32, name="row_sq")
 
         banks = {}
@@ -72,14 +75,14 @@ def tile_qwen2mlp_nd_t_kernel(tc, hidden_state, w_gate, w_up, w_down, out_0, out
         codes = {}
         planes = {}
 
-        def transposes(key, raw, pairs_apart):
+        def transposes(key, raw, pairs_apart, tag="xt"):
             words = raw[:].bitcast(F32)
             if pairs_apart:
                 view = words.rearrange("p (r q u) -> p r u q", r=NT, u=2)
             else:
                 view = words.rearrange("p (r u q) -> p r u q", r=NT, u=2)
             for c in range(2):
-                bank = psum.tile([P, 2, 2 * P], F32, name="xt", tag="xt")
+                bank = psum.tile([P, 2, 2 * P], F32, name=tag, tag=tag)
                 for rr in range(2):
                     for u in range(2):
                         nc.tensor.transpose(bank[:, u, rr * P:(rr + 1) * P], view[:, 2 * c + rr, u, :], ident[:])
@@ -141,7 +144,7 @@ def tile_qwen2mlp_nd_t_kernel(tc, hidden_state, w_gate, w_up, w_down, out_0, out
             if not ok(b):
                 return
             junk = work.tile([P, S], BF16, name="junk", tag="junk")
-            nc.scalar.activation(out=junk[:], in_=hf[b][:, t, :], func=ACT.Square, accum_out=ssum[:, t, b:b + 1])
+            nc.scalar.activation(out=junk[:], in_=hf[b][:, t, :], func=ACT.Square, accum_out=ssum[:, b, t:t + 1])
 
         def cast(b):
             if not ok(b):
@@ -161,10 +164,10 @@ def tile_qwen2mlp_nd_t_kernel(tc, hidden_state, w_gate, w_up, w_down, out_0, out
 
         ob = {}
 
-        def pass2(b, j):
+        def pass2(b, j, tag="ps_o"):
             if not ok(b):
                 return
-            bank = psum.tile([P, H], F32, name="ps_o", tag="ps_o")
+            bank = psum.tile([P, H], F32, name=tag, tag=tag)
             cols = slice(j * P, (j + 1) * P)
             nc.tensor.matmul_mx(
                 out=bank[:],
@@ -173,13 +176,13 @@ def tile_qwen2mlp_nd_t_kernel(tc, hidden_state, w_gate, w_up, w_down, out_0, out
                 start=True, stop=True)
             acc[("o", b, j)] = bank
 
-        def evac_o(b, j):
+        def evac_o(b, j, on_scalar=False):
             if not ok(b):
                 return
             if j == 0:
                 o_sb = work.tile([P, NT, H], F32, name="o_sb", tag="o_sb", bufs=3)
                 ob[b] = o_sb
-            if b == NB - 1 and j % 2 == 1:
+            if on_scalar:
                 nc.scalar.copy(out=ob[b][:, j, :], in_=acc[("o", b, j)][:])
             else:
                 nc.vector.tensor_copy(out=ob[b][:, j, :], in_=acc[("o", b, j)][:])
@@ -192,80 +195,102 @@ def tile_qwen2mlp_nd_t_kernel(tc, hidden_state, w_gate, w_up, w_down, out_0, out
             if ok(b):
                 transposes(b, x_sb[b], False)
 
-        def prep_x_e(b):
-            if ok(b):
-                evacuate(b, 0, True)
-                evacuate(b, 1, True)
+        def impact(b):
+            if not ok(b):
+                return
+            prod = work.tile([P, NT], F32, name="prod", tag="prod")
+            nc.gpsimd.tensor_tensor(out=prod[:], in0=ssum[:, b, :], in1=row_sq[:], op=ALU.mult)
+            nc.gpsimd.tensor_tensor(out=imp_pad[:, :, b], in0=prod[:], in1=half[:], op=ALU.pow)
+
+        wu3 = w_sb["u"][:].rearrange("p (t k) -> p t k", t=NT)
+
+        def row_square(t):
+            junk = work.tile([P, S], BF16, name="junk", tag="junk")
+            nc.scalar.activation(out=junk[:], in_=wu3[:, t, :], func=ACT.Square, accum_out=row_sq[:, t:t + 1])
 
         def prep_x_q(b):
             if ok(b):
                 quantise(b, work, 3, "x")
 
-        def head_group(key, raw, pairs_apart, is_weight):
-            transposes(key, raw, pairs_apart)
-            evacuate(key, 0, True)
-            evacuate(key, 1, False)
-            if is_weight:
-                quantise(key, const, 1, "w" + key)
-            else:
-                quantise(key, work, 3, "x")
+        transposes(0, x_sb[0], False)
+        evacuate(0, 0, True)
+        evacuate(0, 1, False)
+        quantise(0, work, 3, "x")
+        transposes("g", w_sb["g"], False)
+        evacuate("g", 0, True)
+        evacuate("g", 1, False)
+        quantise("g", const, 1, "wg")
+        pass1(0, 0, "g")
+        pass1(0, 1, "g")
+        row_square(0)
+        row_square(1)
+        transposes("u", w_sb["u"], False)
+        evacuate("u", 0, True)
+        evacuate("u", 1, False)
+        quantise("u", const, 1, "wu")
+        pass1(0, 0, "u")
+        pass1(0, 1, "u")
+        prep_x_t(1)
 
-        head_group(0, x_sb[0], False, False)
-        head_group("g", w_sb["g"], False, True)
-        head_group("u", w_sb["u"], False, True)
-        for t in range(2):
-            pass1(0, t, "g")
-            pass1(0, t, "u")
-        wu3 = w_sb["u"][:].rearrange("p (t k) -> p t k", t=NT)
-        for t in range(NT):
-            junk = work.tile([P, S], BF16, name="junk", tag="junk")
-            nc.scalar.activation(out=junk[:], in_=wu3[:, t, :], func=ACT.Square, accum_out=row_sq[:, t:t + 1])
-        head_group(1, x_sb[1], False, False)
-        head_group("d", w_sb["d"], True, True)
-        prep_x_t(2)
-
-        for i in range(NB + 1):
-            silu(i, 0)
-            pass1(i, 2, "g")
-            mult(i, 0)
-            silu(i, 1)
-            pass1(i, 2, "u")
-            pass1(i, 3, "g")
-            mult(i, 1)
-            pass1(i, 3, "u")
-            silu(i, 2)
-            quant_h(i - 1)
-            silu(i, 3)
-            pass2(i - 1, 0)
-            pass2(i - 1, 1)
-            mult(i, 2)
-            pass1(i + 1, 0, "g")
-            pass1(i + 1, 0, "u")
-            mult(i, 3)
-            cast(i)
-            pass1(i + 1, 1, "g")
-            pass1(i + 1, 1, "u")
-            prep_x_e(i + 2)
-            evac_o(i - 1, 0)
-            evac_o(i - 1, 1)
-            if i == NB:
-                store(i - 1, 0, 2)
-            pass2(i - 1, 2)
-            pass2(i - 1, 3)
-            evac_o(i - 1, 2)
-            evac_o(i - 1, 3)
-            if i == NB:
-                store(i - 1, 2, 4)
-            else:
-                store(i - 1, 0, 4)
-            prep_x_t(i + 3)
+        for i in range(NB):
             for t in range(NT):
-                square(i, t)
-            if i == NB - 1:
-                for t in range(NT):
-                    nc.scalar.activation(out=imp_pad[:, t, 0:NB], in_=ssum[:, t, :], func=ACT.Sqrt,
-                                         scale=row_sq[:, t:t + 1])
-            prep_x_q(i + 2)
+                n = NT * i + t
+                silu(i, t)
+                pass1((n + 2) // NT, (n + 2) % NT, "g")
+                if n < 2:
+                    row_square(2 + n)
+                else:
+                    square((n - 2) // NT, (n - 2) % NT)
+                if t == 1:
+                    impact(i - 1)
+                if t == 0 and i >= 1 and ok(i + 1):
+                    evacuate(i + 1, 1, True)
+                if t == 3 and ok(i + 2):
+                    evacuate(i + 2, 0, True)
+                mult(i, t)
+                if t == 3:
+                    cast(i)
+                pass1((n + 2) // NT, (n + 2) % NT, "u")
+                if i == 0 and t < 2:
+                    evacuate(1, t, False)
+                elif i == 0:
+                    evacuate("d", t - 2, False)
+                elif n >= 7:
+                    evac_o((n - 7) // NT, (n - 7) % NT)
+                    if (n - 7) % NT == 3:
+                        store((n - 7) // NT, 0, 4)
+                if n >= 5 and (n - 5) % NT != 0:
+                    pass2((n - 5) // NT, (n - 5) % NT)
+                if t == 1:
+                    prep_x_t(i + 2)
+                    if i == 0:
+                        transposes("d", w_sb["d"], True, "ps_o")
+                    if i == 1:
+                        quantise("d", const, 1, "wd")
+                    quant_h(i - 1)
+                    pass2(i - 1, 0)
+                    prep_x_q(i + 1)
+
+        L = NB - 1
+        square(L, 2)
+        square(L, 3)
+        impact(L)
+        evac_o(L - 1, 1, True)
+        pass2(L - 1, 3)
+        quant_h(L)
+        pass2(L, 0, "ps_g")
+        pass2(L, 1, "ps_u")
+        pass2(L, 2, "ps_g")
+        pass2(L, 3, "ps_u")
+        evac_o(L - 1, 2)
+        evac_o(L - 1, 3, True)
+        store(L - 1, 0, 4)
+        evac_o(L, 0)
+        evac_o(L, 1, True)
+        store(L, 0, 2)
+        evac_o(L, 2)
+        evac_o(L, 3, True)
+        store(L, 2, 4)
 
         imp_t = psum.tile([P, NT, P], F32, name="imp_t", tag="xt")
         for t in range(NT):

@@ -58,15 +58,13 @@ def tile_qwen2mlp_nd_t_kernel(tc, hidden_state, w_gate, w_up, w_down, out_0, out
             load_x(b)
 
         warm = const.tile([P, 2], F32, name="warm")
-        nc.vector.memset(warm[:, 0:1], 0.0)
+        nc.vector.memset(warm[:, 0:1], 1.0)
         nc.scalar.activation(out=warm[:, 1:2], in_=warm[:, 0:1], func=ACT.Silu)
 
         ident = const.tile([P, P], F32, name="ident")
         make_identity(nc, ident[:])
         imp_pad = const.tile([P, NT, P], F32, name="imp_pad")
         nc.gpsimd.memset(imp_pad[:], 0.0)
-        half = const.tile([P, NT], F32, name="half")
-        nc.gpsimd.memset(half[:], 0.5)
         ssum = const.tile([P, NB, NT], F32, name="ssum")
         row_sq = const.tile([P, NT], F32, name="row_sq")
 
@@ -90,7 +88,7 @@ def tile_qwen2mlp_nd_t_kernel(tc, hidden_state, w_gate, w_up, w_down, out_0, out
 
         def evacuate(key, c, on_scalar):
             if c == 0:
-                grp = work.tile([P, 4 * S], BF16, name="grp", tag="grp", align_bytes=64)
+                grp = work.tile([P, 4 * S], BF16, name="grp", tag="grp", bufs=3, align_bytes=64)
                 grouped[key] = grp
             dst = grouped[key][:].bitcast(F32).rearrange("p (s u) -> p s u", u=2)[:, c * 2 * P:(c + 1) * 2 * P, :]
             src = banks[(key, c)][:].rearrange("p u s -> p s u")
@@ -195,13 +193,6 @@ def tile_qwen2mlp_nd_t_kernel(tc, hidden_state, w_gate, w_up, w_down, out_0, out
             if ok(b):
                 transposes(b, x_sb[b], False)
 
-        def impact(b):
-            if not ok(b):
-                return
-            prod = work.tile([P, NT], F32, name="prod", tag="prod")
-            nc.gpsimd.tensor_tensor(out=prod[:], in0=ssum[:, b, :], in1=row_sq[:], op=ALU.mult)
-            nc.gpsimd.tensor_tensor(out=imp_pad[:, :, b], in0=prod[:], in1=half[:], op=ALU.pow)
-
         wu3 = w_sb["u"][:].rearrange("p (t k) -> p t k", t=NT)
 
         def row_square(t):
@@ -213,88 +204,101 @@ def tile_qwen2mlp_nd_t_kernel(tc, hidden_state, w_gate, w_up, w_down, out_0, out
                 quantise(b, work, 3, "x")
 
         transposes(0, x_sb[0], False)
+        transposes("g", w_sb["g"], False, "ps_o")
         evacuate(0, 0, True)
         evacuate(0, 1, False)
         quantise(0, work, 3, "x")
-        transposes("g", w_sb["g"], False)
+        transposes("u", w_sb["u"], False)
         evacuate("g", 0, True)
         evacuate("g", 1, False)
         quantise("g", const, 1, "wg")
         pass1(0, 0, "g")
         pass1(0, 1, "g")
-        row_square(0)
-        row_square(1)
-        transposes("u", w_sb["u"], False)
+        transposes(1, x_sb[1], False, "ps_o")
         evacuate("u", 0, True)
         evacuate("u", 1, False)
         quantise("u", const, 1, "wu")
         pass1(0, 0, "u")
         pass1(0, 1, "u")
-        prep_x_t(1)
+        transposes(2, x_sb[2], False)
+        evacuate(1, 0, True)
+        evacuate(1, 1, False)
 
         for i in range(NB):
             for t in range(NT):
                 n = NT * i + t
                 silu(i, t)
                 pass1((n + 2) // NT, (n + 2) % NT, "g")
+                if n == NT * NB - 1:
+                    nc.scalar.activation(out=warm[:, 1:2], in_=warm[:, 0:1], func=ACT.Sqrt)
                 if n < 2:
-                    row_square(2 + n)
+                    row_square(n)
                 else:
                     square((n - 2) // NT, (n - 2) % NT)
-                if t == 1:
-                    impact(i - 1)
-                if t == 0 and i >= 1 and ok(i + 1):
-                    evacuate(i + 1, 1, True)
-                if t == 3 and ok(i + 2):
-                    evacuate(i + 2, 0, True)
+                if t == 0 and i >= 1:
+                    if ok(i + 2):
+                        evacuate(i + 2, 1, True)
+                    elif i == NB - 2:
+                        row_square(3)
+                if t == 3:
+                    if ok(i + 3):
+                        evacuate(i + 3, 0, True)
+                    elif i == NB - 3:
+                        row_square(2)
                 mult(i, t)
                 if t == 3:
                     cast(i)
                 pass1((n + 2) // NT, (n + 2) % NT, "u")
-                if i == 0 and t < 2:
-                    evacuate(1, t, False)
-                elif i == 0:
-                    evacuate("d", t - 2, False)
+                if i == 0:
+                    if t == 0:
+                        prep_x_q(1)
+                        transposes("d", w_sb["d"], True, "ps_o")
+                        evacuate(2, 0, False)
+                    elif t == 1:
+                        evacuate(2, 1, False)
+                    else:
+                        evacuate("d", t - 2, False)
                 elif n >= 7:
                     evac_o((n - 7) // NT, (n - 7) % NT)
                     if (n - 7) % NT == 3:
                         store((n - 7) // NT, 0, 4)
-                if n >= 5 and (n - 5) % NT != 0:
+                if n >= 7 and (n - 5) % NT >= 2:
                     pass2((n - 5) // NT, (n - 5) % NT)
                 if t == 1:
-                    prep_x_t(i + 2)
-                    if i == 0:
-                        transposes("d", w_sb["d"], True, "ps_o")
+                    prep_x_t(i + 3)
+                if t == 2:
                     if i == 1:
                         quantise("d", const, 1, "wd")
                     quant_h(i - 1)
                     pass2(i - 1, 0)
-                    prep_x_q(i + 1)
+                    pass2(i - 1, 1)
+                    prep_x_q(i + 2)
 
         L = NB - 1
         square(L, 2)
         square(L, 3)
-        impact(L)
-        evac_o(L - 1, 1, True)
-        pass2(L - 1, 3)
+        for t in range(NT):
+            nc.scalar.activation(out=imp_pad[:, t, 0:NB], in_=ssum[:, :, t], func=ACT.Sqrt, scale=row_sq[:, t:t + 1])
         quant_h(L)
-        pass2(L, 0, "ps_g")
-        pass2(L, 1, "ps_u")
-        pass2(L, 2, "ps_g")
-        pass2(L, 3, "ps_u")
+        pass2(L - 1, 3, "ps_g")
+        imp_t = psum.tile([P, NT, P], F32, name="imp_t", tag="xt")
+        for t in range(NT):
+            nc.tensor.transpose(imp_t[:, t, :], imp_pad[:, t, :], ident[:])
+        pass2(L, 0, "ps_u")
+        pass2(L, 1, "ps_g")
+        pass2(L, 2, "ps_u")
+        evac_o(L - 1, 1, True)
+        store(L - 1, 0, 2)
         evac_o(L - 1, 2)
-        evac_o(L - 1, 3, True)
-        store(L - 1, 0, 4)
+        imp_sb = const.tile([P, P, NT], F32, name="imp_sb")
+        nc.scalar.copy(out=imp_sb[:], in_=imp_t[:].rearrange("c t p -> c p t"))
+        nc.sync.dma_start(out=out_1, in_=imp_sb[0:NB].rearrange("c p t -> c (p t)"))
+        evac_o(L - 1, 3)
+        store(L - 1, 2, 4)
+        pass2(L, 3, "ps_o")
         evac_o(L, 0)
         evac_o(L, 1, True)
         store(L, 0, 2)
         evac_o(L, 2)
         evac_o(L, 3, True)
         store(L, 2, 4)
-
-        imp_t = psum.tile([P, NT, P], F32, name="imp_t", tag="xt")
-        for t in range(NT):
-            nc.tensor.transpose(imp_t[:, t, :], imp_pad[:, t, :], ident[:])
-        imp_sb = const.tile([P, P, NT], F32, name="imp_sb")
-        nc.scalar.copy(out=imp_sb[:], in_=imp_t[:].rearrange("c t p -> c p t"))
-        nc.sync.dma_start(out=out_1, in_=imp_sb[0:NB].rearrange("c p t -> c (p t)"))

@@ -21,6 +21,8 @@ FLOPS = 3 * 2 * NB * S * H * I
 
 PINNED = True
 GP_CAST = True
+WARM_FIRST = 9
+WARM_BETWEEN = 2
 
 
 def tile_qwen2mlp_nd_t_kernel(tc, hidden_state, w_gate, w_up, w_down, out_0, out_1):
@@ -203,36 +205,52 @@ def tile_qwen2mlp_nd_t_kernel(tc, hidden_state, w_gate, w_up, w_down, out_0, out
             if ok(b):
                 quantise(b, work, 3, "x")
 
+        zeros = const.tile([P, S], BF16, name="zeros")
+        nc.vector.memset(zeros[:], 0.0)
+
+        def keep_warm(count):
+            for q in range(count):
+                bank = psum.tile([P, S], F32, name="ps_u", tag="ps_u")
+                nc.tensor.matmul(out=bank[:], lhsT=zeros[:, 0:P], rhs=zeros[:], start=True, stop=True)
+
+        keep_warm(WARM_FIRST)
         transposes(0, x_sb[0], False)
+        keep_warm(WARM_BETWEEN)
         transposes("g", w_sb["g"], False, "ps_o")
+        keep_warm(WARM_BETWEEN)
         evacuate(0, 0, True)
         evacuate(0, 1, False)
         quantise(0, work, 3, "x")
         transposes("u", w_sb["u"], False)
+        keep_warm(WARM_BETWEEN)
         evacuate("g", 0, True)
         evacuate("g", 1, False)
         quantise("g", const, 1, "wg")
+        transposes(1, x_sb[1], False, "ps_o")
         pass1(0, 0, "g")
         pass1(0, 1, "g")
-        transposes(1, x_sb[1], False, "ps_o")
+        row_square(0)
         evacuate("u", 0, True)
         evacuate("u", 1, False)
         quantise("u", const, 1, "wu")
+        row_square(1)
         pass1(0, 0, "u")
         pass1(0, 1, "u")
         transposes(2, x_sb[2], False)
-        evacuate(1, 0, True)
-        evacuate(1, 1, False)
 
+        L = NB - 1
+        LAST = NT * NB - 1
         for i in range(NB):
             for t in range(NT):
                 n = NT * i + t
                 silu(i, t)
                 pass1((n + 2) // NT, (n + 2) % NT, "g")
-                if n == NT * NB - 1:
+                if n == LAST:
+                    pass2(L - 1, 2, "ps_g")
+                    pass2(L - 1, 3, "ps_g")
                     nc.scalar.activation(out=warm[:, 1:2], in_=warm[:, 0:1], func=ACT.Sqrt)
                 if n < 2:
-                    row_square(n)
+                    evacuate(1, n, True)
                 else:
                     square((n - 2) // NT, (n - 2) % NT)
                 if t == 0 and i >= 1:
@@ -248,22 +266,23 @@ def tile_qwen2mlp_nd_t_kernel(tc, hidden_state, w_gate, w_up, w_down, out_0, out
                 mult(i, t)
                 if t == 3:
                     cast(i)
+                if n == 1:
+                    prep_x_q(1)
                 pass1((n + 2) // NT, (n + 2) % NT, "u")
                 if i == 0:
-                    if t == 0:
-                        prep_x_q(1)
+                    if t < 2:
+                        evacuate(2, t, False)
+                    if t == 1:
                         transposes("d", w_sb["d"], True, "ps_o")
-                        evacuate(2, 0, False)
-                    elif t == 1:
-                        evacuate(2, 1, False)
-                    else:
+                    if t >= 2:
                         evacuate("d", t - 2, False)
-                elif n >= 7:
-                    evac_o((n - 7) // NT, (n - 7) % NT)
-                    if (n - 7) % NT == 3:
-                        store((n - 7) // NT, 0, 4)
-                if n >= 7 and (n - 5) % NT >= 2:
-                    pass2((n - 5) // NT, (n - 5) % NT)
+                elif 7 <= n < LAST:
+                    b, j = divmod(n - 7, NT)
+                    evac_o(b, j)
+                    if j % 2 == 1:
+                        store(b, j - 1, j + 1)
+                    if j < 2:
+                        pass2(b, j + 2)
                 if t == 1:
                     prep_x_t(i + 3)
                 if t == 2:
@@ -274,31 +293,29 @@ def tile_qwen2mlp_nd_t_kernel(tc, hidden_state, w_gate, w_up, w_down, out_0, out
                     pass2(i - 1, 1)
                     prep_x_q(i + 2)
 
-        L = NB - 1
+        quant_h(L)
+        evac_o(L - 1, 0, True)
+        evac_o(L - 1, 1, True)
+        store(L - 1, 0, 2)
+        pass2(L, 0, "ps_u")
+        pass2(L, 1, "ps_u")
+        pass2(L, 2, "ps_o")
+        pass2(L, 3, "ps_o")
+        evac_o(L - 1, 2, True)
+        evac_o(L - 1, 3)
+        store(L - 1, 2, 4)
         square(L, 2)
         square(L, 3)
         for t in range(NT):
             nc.scalar.activation(out=imp_pad[:, t, 0:NB], in_=ssum[:, :, t], func=ACT.Sqrt, scale=row_sq[:, t:t + 1])
-        quant_h(L)
-        pass2(L - 1, 3, "ps_g")
         imp_t = psum.tile([P, NT, P], F32, name="imp_t", tag="xt")
         for t in range(NT):
             nc.tensor.transpose(imp_t[:, t, :], imp_pad[:, t, :], ident[:])
-        pass2(L, 0, "ps_u")
-        pass2(L, 1, "ps_g")
-        pass2(L, 2, "ps_u")
-        evac_o(L - 1, 1, True)
-        store(L - 1, 0, 2)
-        evac_o(L - 1, 2)
+        for j in range(3):
+            evac_o(L, j)
+            store(L, j, j + 1)
+        evac_o(L, 3, True)
+        store(L, 3, 4)
         imp_sb = const.tile([P, P, NT], F32, name="imp_sb")
         nc.scalar.copy(out=imp_sb[:], in_=imp_t[:].rearrange("c t p -> c p t"))
         nc.sync.dma_start(out=out_1, in_=imp_sb[0:NB].rearrange("c p t -> c (p t)"))
-        evac_o(L - 1, 3)
-        store(L - 1, 2, 4)
-        pass2(L, 3, "ps_o")
-        evac_o(L, 0)
-        evac_o(L, 1, True)
-        store(L, 0, 2)
-        evac_o(L, 2)
-        evac_o(L, 3, True)
-        store(L, 2, 4)

@@ -21,8 +21,8 @@ FLOPS = 3 * 2 * NB * S * H * I
 
 PINNED = True
 GP_CAST = True
-WARM_FIRST = 9
-WARM_BETWEEN = 2
+WARM_FIRST = 4
+WARM_BETWEEN = 1
 
 
 def tile_qwen2mlp_nd_t_kernel(tc, hidden_state, w_gate, w_up, w_down, out_0, out_1):
@@ -40,24 +40,28 @@ def tile_qwen2mlp_nd_t_kernel(tc, hidden_state, w_gate, w_up, w_down, out_0, out
         x_sb = {}
         w_sb = {}
 
-        def load_x(b):
+        def load(raw, view, r0, r1):
+            nc.sync.dma_start(out=raw[:].rearrange("p (r k) -> p r k", r=NT)[:, r0:r1, :], in_=view[:, r0:r1, :])
+
+        for b in range(NB):
             x_raw = xin.tile([P, NT * H], BF16, name="x_raw")
-            nc.sync.dma_start(out=x_raw[:].rearrange("p (j h) -> p j h", j=NT), in_=x_view[b])
             x_sb[b] = x_raw
-
-        def load_w(key, view):
+        for key in ("g", "u", "d"):
             w_raw = const.tile([P, NT * H], BF16, name="w_raw_" + key)
-            nc.sync.dma_start(out=w_raw[:].rearrange("p (r k) -> p r k", r=NT), in_=view)
             w_sb[key] = w_raw
-
-        load_x(0)
-        load_w("g", w_gate.rearrange("(p t) k -> p t k", t=NT))
-        load_w("u", w_up.rearrange("(p t) k -> p t k", t=NT))
-        load_x(1)
-        load_x(2)
-        load_w("d", w_down.rearrange("(r p) k -> p r k", p=P))
+        g_view = w_gate.rearrange("(p t) k -> p t k", t=NT)
+        u_view = w_up.rearrange("(p t) k -> p t k", t=NT)
+        load(x_sb[0], x_view[0], 0, 2)
+        load(x_sb[0], x_view[0], 2, 4)
+        load(w_sb["g"], g_view, 0, 2)
+        load(w_sb["u"], u_view, 0, 2)
+        load(w_sb["g"], g_view, 2, 4)
+        load(w_sb["u"], u_view, 2, 4)
+        load(x_sb[1], x_view[1], 0, 4)
+        load(x_sb[2], x_view[2], 0, 4)
+        load(w_sb["d"], w_down.rearrange("(r p) k -> p r k", p=P), 0, 4)
         for b in range(3, NB):
-            load_x(b)
+            load(x_sb[b], x_view[b], 0, 4)
 
         warm = const.tile([P, 2], F32, name="warm")
         nc.vector.memset(warm[:, 0:1], 1.0)
@@ -75,13 +79,13 @@ def tile_qwen2mlp_nd_t_kernel(tc, hidden_state, w_gate, w_up, w_down, out_0, out
         codes = {}
         planes = {}
 
-        def transposes(key, raw, pairs_apart, tag="xt"):
+        def transposes(key, raw, pairs_apart, tag="xt", halves=(0, 1)):
             words = raw[:].bitcast(F32)
             if pairs_apart:
                 view = words.rearrange("p (r q u) -> p r u q", r=NT, u=2)
             else:
                 view = words.rearrange("p (r u q) -> p r u q", r=NT, u=2)
-            for c in range(2):
+            for c in halves:
                 bank = psum.tile([P, 2, 2 * P], F32, name=tag, tag=tag)
                 for rr in range(2):
                     for u in range(2):
@@ -89,7 +93,7 @@ def tile_qwen2mlp_nd_t_kernel(tc, hidden_state, w_gate, w_up, w_down, out_0, out
                 banks[(key, c)] = bank
 
         def evacuate(key, c, on_scalar):
-            if c == 0:
+            if key not in grouped:
                 grp = work.tile([P, 4 * S], BF16, name="grp", tag="grp", bufs=3, align_bytes=64)
                 grouped[key] = grp
             dst = grouped[key][:].bitcast(F32).rearrange("p (s u) -> p s u", u=2)[:, c * 2 * P:(c + 1) * 2 * P, :]
@@ -99,12 +103,14 @@ def tile_qwen2mlp_nd_t_kernel(tc, hidden_state, w_gate, w_up, w_down, out_0, out
             else:
                 nc.vector.tensor_copy(out=dst, in_=src)
 
-        def quantise(key, pool, bufs, tag):
-            cod = pool.tile([P, S], U32, name="cod_" + tag, tag="cod_" + tag, bufs=bufs, align_bytes=64)
-            pla = pool.tile([P, S], U8, name="pla_" + tag, tag="pla_" + tag, bufs=bufs, align_bytes=64)
-            nc.vector.quantize_mx(out=cod[:].bitcast(FP8X4), scales=pla[:], in_=grouped[key][:])
-            codes[key] = cod
-            planes[key] = pla
+        def quantise(key, pool, bufs, tag, c0=0, c1=S):
+            if key not in codes:
+                cod = pool.tile([P, S], U32, name="cod_" + tag, tag="cod_" + tag, bufs=bufs, align_bytes=64)
+                pla = pool.tile([P, S], U8, name="pla_" + tag, tag="pla_" + tag, bufs=bufs, align_bytes=64)
+                codes[key] = cod
+                planes[key] = pla
+            nc.vector.quantize_mx(out=codes[key][:, c0:c1].bitcast(FP8X4), scales=planes[key][:, c0:c1],
+                                  in_=grouped[key][:, 4 * c0:4 * c1])
 
         def ok(b):
             return 0 <= b < NB
@@ -213,34 +219,67 @@ def tile_qwen2mlp_nd_t_kernel(tc, hidden_state, w_gate, w_up, w_down, out_0, out
                 bank = psum.tile([P, S], F32, name="ps_u", tag="ps_u")
                 nc.tensor.matmul(out=bank[:], lhsT=zeros[:, 0:P], rhs=zeros[:], start=True, stop=True)
 
+        HALF = S // 2
         keep_warm(WARM_FIRST)
         transposes(0, x_sb[0], False)
         keep_warm(WARM_BETWEEN)
-        transposes("g", w_sb["g"], False, "ps_o")
+        transposes("g", w_sb["g"], False, "ps_o", (0,))
+        transposes("u", w_sb["u"], False, "ps_o", (0,))
         keep_warm(WARM_BETWEEN)
         evacuate(0, 0, True)
         evacuate(0, 1, False)
         quantise(0, work, 3, "x")
-        transposes("u", w_sb["u"], False)
-        keep_warm(WARM_BETWEEN)
+        transposes("g", w_sb["g"], False, "xt", (1,))
         evacuate("g", 0, True)
-        evacuate("g", 1, False)
-        quantise("g", const, 1, "wg")
-        transposes(1, x_sb[1], False, "ps_o")
+        quantise("g", const, 1, "wg", 0, HALF)
         pass1(0, 0, "g")
         pass1(0, 1, "g")
-        row_square(0)
         evacuate("u", 0, True)
-        evacuate("u", 1, False)
-        quantise("u", const, 1, "wu")
-        row_square(1)
+        quantise("u", const, 1, "wu", 0, HALF)
         pass1(0, 0, "u")
         pass1(0, 1, "u")
+        transposes("u", w_sb["u"], False, "xt", (1,))
+        evacuate("g", 1, True)
+        quantise("g", const, 1, "wg", HALF, S)
+        transposes(1, x_sb[1], False, "ps_o")
+
+        silu(0, 0)
+        pass1(0, 2, "g")
+        row_square(0)
+        mult(0, 0)
+        evacuate("u", 1, False)
+        quantise("u", const, 1, "wu", HALF, S)
+        pass1(0, 2, "u")
         transposes(2, x_sb[2], False)
+        silu(0, 1)
+        pass1(0, 3, "g")
+        evacuate(1, 0, True)
+        mult(0, 1)
+        pass1(0, 3, "u")
+        evacuate(1, 1, False)
+        prep_x_q(1)
+        transposes("d", w_sb["d"], True, "ps_o")
+        silu(0, 2)
+        pass1(1, 0, "g")
+        square(0, 0)
+        row_square(1)
+        mult(0, 2)
+        pass1(1, 0, "u")
+        evacuate(2, 0, False)
+        evacuate(2, 1, False)
+        prep_x_t(3)
+        prep_x_q(2)
+        silu(0, 3)
+        pass1(1, 1, "g")
+        square(0, 1)
+        evacuate(3, 0, True)
+        mult(0, 3)
+        cast(0)
+        pass1(1, 1, "u")
 
         L = NB - 1
         LAST = NT * NB - 1
-        for i in range(NB):
+        for i in range(1, NB):
             for t in range(NT):
                 n = NT * i + t
                 silu(i, t)
@@ -249,11 +288,8 @@ def tile_qwen2mlp_nd_t_kernel(tc, hidden_state, w_gate, w_up, w_down, out_0, out
                     pass2(L - 1, 2, "ps_g")
                     pass2(L - 1, 3, "ps_g")
                     nc.scalar.activation(out=warm[:, 1:2], in_=warm[:, 0:1], func=ACT.Sqrt)
-                if n < 2:
-                    evacuate(1, n, True)
-                else:
-                    square((n - 2) // NT, (n - 2) % NT)
-                if t == 0 and i >= 1:
+                square((n - 2) // NT, (n - 2) % NT)
+                if t == 0:
                     if ok(i + 2):
                         evacuate(i + 2, 1, True)
                     elif i == NB - 2:
@@ -266,16 +302,9 @@ def tile_qwen2mlp_nd_t_kernel(tc, hidden_state, w_gate, w_up, w_down, out_0, out
                 mult(i, t)
                 if t == 3:
                     cast(i)
-                if n == 1:
-                    prep_x_q(1)
                 pass1((n + 2) // NT, (n + 2) % NT, "u")
-                if i == 0:
-                    if t < 2:
-                        evacuate(2, t, False)
-                    if t == 1:
-                        transposes("d", w_sb["d"], True, "ps_o")
-                    if t >= 2:
-                        evacuate("d", t - 2, False)
+                if i == 1 and t < 2:
+                    evacuate("d", t, False)
                 elif 7 <= n < LAST:
                     b, j = divmod(n - 7, NT)
                     evac_o(b, j)

@@ -272,7 +272,6 @@ def tile_qwen2mlp_nd_t_kernel(tc, hidden_state, w_gate, w_up, w_down, out_0, out
         silu(0, 3)
         pass1(1, 1, "g")
         square(0, 1)
-        evacuate(3, 0, True)
         mult(0, 3)
         cast(0)
         pass1(1, 1, "u")
@@ -289,7 +288,10 @@ def tile_qwen2mlp_nd_t_kernel(tc, hidden_state, w_gate, w_up, w_down, out_0, out
                     pass2(L - 1, 3, "ps_g")
                     nc.scalar.activation(out=warm[:, 1:2], in_=warm[:, 0:1], func=ACT.Sqrt)
                 square((n - 2) // NT, (n - 2) % NT)
-                if t == 0:
+                if i == 1:
+                    if t < 2:
+                        evacuate(3, t, True)
+                elif t == 0:
                     if ok(i + 2):
                         evacuate(i + 2, 1, True)
                     elif i == NB - 2:
@@ -346,5 +348,5 @@ def tile_qwen2mlp_nd_t_kernel(tc, hidden_state, w_gate, w_up, w_down, out_0, out
         evac_o(L, 3, True)
         store(L, 3, 4)
         imp_sb = const.tile([P, P, NT], F32, name="imp_sb")
-        nc.scalar.copy(out=imp_sb[:], in_=imp_t[:].rearrange("c t p -> c p t"))
+        nc.vector.tensor_copy(out=imp_sb[:], in_=imp_t[:].rearrange("c t p -> c p t"))
         nc.sync.dma_start(out=out_1, in_=imp_sb[0:NB].rearrange("c p t -> c (p t)"))

@@ -230,6 +230,7 @@ def tile_qwen2mlp_nd_t_kernel(tc, hidden_state, w_gate, w_up, w_down, out_0, out
         evacuate(0, 1, False)
         quantise(0, work, 3, "x")
         transposes("g", w_sb["g"], False, "xt", (1,))
+        transposes("u", w_sb["u"], False, "xt", (1,))
         evacuate("g", 0, True)
         quantise("g", const, 1, "wg", 0, HALF)
         pass1(0, 0, "g")
@@ -238,17 +239,16 @@ def tile_qwen2mlp_nd_t_kernel(tc, hidden_state, w_gate, w_up, w_down, out_0, out
         quantise("u", const, 1, "wu", 0, HALF)
         pass1(0, 0, "u")
         pass1(0, 1, "u")
-        transposes("u", w_sb["u"], False, "xt", (1,))
+        evacuate("u", 1, False)
         evacuate("g", 1, True)
         quantise("g", const, 1, "wg", HALF, S)
+        quantise("u", const, 1, "wu", HALF, S)
         transposes(1, x_sb[1], False, "ps_o")
 
         silu(0, 0)
         pass1(0, 2, "g")
         row_square(0)
         mult(0, 0)
-        evacuate("u", 1, False)
-        quantise("u", const, 1, "wu", HALF, S)
         pass1(0, 2, "u")
         transposes(2, x_sb[2], False)
         silu(0, 1)
@@ -262,11 +262,10 @@ def tile_qwen2mlp_nd_t_kernel(tc, hidden_state, w_gate, w_up, w_down, out_0, out
         silu(0, 2)
         pass1(1, 0, "g")
         square(0, 0)
-        row_square(1)
+        evacuate(2, 1, True)
         mult(0, 2)
         pass1(1, 0, "u")
         evacuate(2, 0, False)
-        evacuate(2, 1, False)
         prep_x_t(3)
         prep_x_q(2)
         silu(0, 3)
@@ -283,13 +282,18 @@ def tile_qwen2mlp_nd_t_kernel(tc, hidden_state, w_gate, w_up, w_down, out_0, out
                 n = NT * i + t
                 silu(i, t)
                 pass1((n + 2) // NT, (n + 2) % NT, "g")
+                if t == 3:
+                    pass2(i - 1, 0)
+                    pass2(i - 1, 1)
                 if n == LAST:
                     pass2(L - 1, 2, "ps_g")
                     pass2(L - 1, 3, "ps_g")
                     nc.scalar.activation(out=warm[:, 1:2], in_=warm[:, 0:1], func=ACT.Sqrt)
                 square((n - 2) // NT, (n - 2) % NT)
+                if n == LAST - NT:
+                    row_square(1)
                 if i == 1:
-                    if t < 2:
+                    if t == 1:
                         evacuate(3, t, True)
                 elif t == 0:
                     if ok(i + 2):
@@ -307,6 +311,8 @@ def tile_qwen2mlp_nd_t_kernel(tc, hidden_state, w_gate, w_up, w_down, out_0, out
                 pass1((n + 2) // NT, (n + 2) % NT, "u")
                 if i == 1 and t < 2:
                     evacuate("d", t, False)
+                    if t == 0:
+                        evacuate(3, t, False)
                 elif 7 <= n < LAST:
                     b, j = divmod(n - 7, NT)
                     evac_o(b, j)
@@ -320,8 +326,6 @@ def tile_qwen2mlp_nd_t_kernel(tc, hidden_state, w_gate, w_up, w_down, out_0, out
                     if i == 1:
                         quantise("d", const, 1, "wd")
                     quant_h(i - 1)
-                    pass2(i - 1, 0)
-                    pass2(i - 1, 1)
                     prep_x_q(i + 2)
 
         quant_h(L)

@@ -18,11 +18,13 @@ H = 512
 I = 512
 NT = 4
 FLOPS = 3 * 2 * NB * S * H * I
+HALF_S = S // 2
 
 PINNED = True
 GP_CAST = True
 WARM_FIRST = 4
 WARM_BETWEEN = 1
+END_FROM = 29
 
 
 def tile_qwen2mlp_nd_t_kernel(tc, hidden_state, w_gate, w_up, w_down, out_0, out_1):
@@ -164,6 +166,18 @@ def tile_qwen2mlp_nd_t_kernel(tc, hidden_state, w_gate, w_up, w_down, out_0, out
             else:
                 nc.vector.tensor_copy(out=dst, in_=src)
 
+        def cast_half(b, c):
+            if c == 0:
+                grp = work.tile([P, 4 * S], BF16, name="hgrp", tag="hgrp", align_bytes=64)
+                grouped[("h", b)] = grp
+            cols = slice(c * HALF_S, (c + 1) * HALF_S)
+            dst = grouped[("h", b)][:].rearrange("p (s t) -> p s t", t=NT)[:, cols, :]
+            src = hf[b][:].rearrange("p t s -> p s t")[:, cols, :]
+            nc.vector.tensor_copy(out=dst, in_=src)
+
+        def quant_h_half(b, c):
+            quantise(("h", b), work, 2, "h", c * HALF_S, (c + 1) * HALF_S)
+
         def quant_h(b):
             if ok(b):
                 quantise(("h", b), work, 2, "h")
@@ -277,80 +291,105 @@ def tile_qwen2mlp_nd_t_kernel(tc, hidden_state, w_gate, w_up, w_down, out_0, out
 
         L = NB - 1
         LAST = NT * NB - 1
-        for i in range(1, NB):
-            for t in range(NT):
-                n = NT * i + t
-                silu(i, t)
-                pass1((n + 2) // NT, (n + 2) % NT, "g")
-                if t == 3:
-                    pass2(i - 1, 0)
-                    pass2(i - 1, 1)
-                if n == LAST:
-                    pass2(L - 1, 2, "ps_g")
-                    pass2(L - 1, 3, "ps_g")
-                    nc.scalar.activation(out=warm[:, 1:2], in_=warm[:, 0:1], func=ACT.Sqrt)
-                square((n - 2) // NT, (n - 2) % NT)
-                if n == LAST - NT:
-                    row_square(1)
-                if i == 1:
-                    if t == 1:
-                        evacuate(3, t, True)
-                elif t == 0:
-                    if ok(i + 2):
-                        evacuate(i + 2, 1, True)
-                    elif i == NB - 2:
-                        row_square(3)
-                if t == 3:
-                    if ok(i + 3):
-                        evacuate(i + 3, 0, True)
-                    elif i == NB - 3:
-                        row_square(2)
-                mult(i, t)
-                if t == 3:
-                    cast(i)
-                pass1((n + 2) // NT, (n + 2) % NT, "u")
-                if i == 1 and t < 2:
-                    evacuate("d", t, False)
-                    if t == 0:
-                        evacuate(3, t, False)
-                elif 7 <= n < LAST:
-                    b, j = divmod(n - 7, NT)
-                    evac_o(b, j)
-                    if j % 2 == 1:
-                        store(b, j - 1, j + 1)
-                    if j < 2:
-                        pass2(b, j + 2)
+        for n in range(NT, END_FROM):
+            i, t = divmod(n, NT)
+            silu(i, t)
+            pass1((n + 2) // NT, (n + 2) % NT, "g")
+            if t == 3:
+                pass2(i - 1, 0)
+                pass2(i - 1, 1)
+            if n == LAST:
+                pass2(L - 1, 2, "ps_g")
+                pass2(L - 1, 3, "ps_g")
+                nc.scalar.activation(out=warm[:, 1:2], in_=warm[:, 0:1], func=ACT.Sqrt)
+            square((n - 2) // NT, (n - 2) % NT)
+            if n == LAST - NT:
+                row_square(1)
+            if i == 1:
                 if t == 1:
-                    prep_x_t(i + 3)
-                if t == 2:
-                    if i == 1:
-                        quantise("d", const, 1, "wd")
-                    quant_h(i - 1)
-                    prep_x_q(i + 2)
+                    evacuate(3, t, True)
+            elif t == 0:
+                if ok(i + 2):
+                    evacuate(i + 2, 1, True)
+                elif i == NB - 2:
+                    row_square(3)
+            if t == 3:
+                if ok(i + 3):
+                    evacuate(i + 3, 0, True)
+                elif i == NB - 3:
+                    row_square(2)
+            mult(i, t)
+            if t == 3:
+                cast(i)
+            pass1((n + 2) // NT, (n + 2) % NT, "u")
+            if i == 1 and t < 2:
+                evacuate("d", t, False)
+                if t == 0:
+                    evacuate(3, t, False)
+            elif 7 <= n < LAST:
+                b, j = divmod(n - 7, NT)
+                evac_o(b, j)
+                if j % 2 == 1:
+                    store(b, j - 1, j + 1)
+                if j < 2:
+                    pass2(b, j + 2)
+            if t == 1:
+                prep_x_t(i + 3)
+            if t == 2:
+                if i == 1:
+                    quantise("d", const, 1, "wd")
+                quant_h(i - 1)
+                prep_x_q(i + 2)
 
-        quant_h(L)
-        evac_o(L - 1, 0, True)
-        evac_o(L - 1, 1, True)
-        store(L - 1, 0, 2)
-        pass2(L, 0, "ps_u")
-        pass2(L, 1, "ps_u")
-        pass2(L, 2, "ps_o")
-        pass2(L, 3, "ps_o")
-        evac_o(L - 1, 2, True)
-        evac_o(L - 1, 3)
-        store(L - 1, 2, 4)
-        square(L, 2)
-        square(L, 3)
+        silu(7, 1)
+        pass1(7, 3, "g")
+        square(6, 3)
+        mult(7, 1)
+        pass1(7, 3, "u")
+        evac_o(5, 2)
+        quant_h(6)
+        silu(7, 2)
+        pass2(6, 0, "xt")
+        pass2(6, 1, "xt")
+        square(7, 0)
+        mult(7, 2)
+        evac_o(5, 3)
+        store(5, 2, 4)
+        silu(7, 3)
+        pass2(6, 2, "ps_g")
+        pass2(6, 3, "ps_g")
+        nc.scalar.activation(out=warm[:, 1:2], in_=warm[:, 0:1], func=ACT.Sqrt)
+        evac_o(6, 0, True)
+        evac_o(6, 1, True)
+        store(6, 0, 2)
+        mult(7, 3)
+        cast_half(7, 0)
+        quant_h_half(7, 0)
+        pass2(7, 0, "ps_u")
+        pass2(7, 1, "ps_u")
+        cast_half(7, 1)
+        quant_h_half(7, 1)
+        pass2(7, 2, "ps_o")
+        pass2(7, 3, "ps_o")
+        evac_o(6, 2, True)
+        evac_o(6, 3, True)
+        store(6, 2, 4)
+        square(7, 1)
+        square(7, 2)
+        square(7, 3)
         for t in range(NT):
             nc.scalar.activation(out=imp_pad[:, t, 0:NB], in_=ssum[:, :, t], func=ACT.Sqrt, scale=row_sq[:, t:t + 1])
         imp_t = psum.tile([P, NT, P], F32, name="imp_t", tag="xt")
         for t in range(NT):
             nc.tensor.transpose(imp_t[:, t, :], imp_pad[:, t, :], ident[:])
-        for j in range(3):
-            evac_o(L, j)
-            store(L, j, j + 1)
-        evac_o(L, 3, True)
-        store(L, 3, 4)
+        evac_o(7, 0)
+        store(7, 0, 1)
+        evac_o(7, 1)
+        store(7, 1, 2)
+        evac_o(7, 2)
+        store(7, 2, 3)
+        evac_o(7, 3)
+        store(7, 3, 4)
         imp_sb = const.tile([P, P, NT], F32, name="imp_sb")
-        nc.vector.tensor_copy(out=imp_sb[:], in_=imp_t[:].rearrange("c t p -> c p t"))
+        nc.scalar.copy(out=imp_sb[:], in_=imp_t[:].rearrange("c t p -> c p t"))
         nc.sync.dma_start(out=out_1, in_=imp_sb[0:NB].rearrange("c p t -> c (p t)"))

@@ -374,13 +374,11 @@ def tile_qwen2mlp_nd_t_kernel(tc, hidden_state, w_gate, w_up, w_down, out_0, out
         evac_o(6, 2, True)
         evac_o(6, 3, True)
         store(6, 2, 4)
-        square(7, 1)
-        square(7, 2)
-        square(7, 3)
-        for t in range(NT):
-            nc.scalar.activation(out=imp_pad[:, t, 0:NB], in_=ssum[:, :, t], func=ACT.Sqrt, scale=row_sq[:, t:t + 1])
         imp_t = psum.tile([P, NT, P], F32, name="imp_t", tag="xt")
         for t in range(NT):
+            if t > 0:
+                square(7, t)
+            nc.scalar.activation(out=imp_pad[:, t, 0:NB], in_=ssum[:, :, t], func=ACT.Sqrt, scale=row_sq[:, t:t + 1])
             nc.tensor.transpose(imp_t[:, t, :], imp_pad[:, t, :], ident[:])
         evac_o(7, 0)
         store(7, 0, 1)
@@ -388,7 +386,7 @@ def tile_qwen2mlp_nd_t_kernel(tc, hidden_state, w_gate, w_up, w_down, out_0, out
         store(7, 1, 2)
         evac_o(7, 2)
         store(7, 2, 3)
-        evac_o(7, 3)
+        evac_o(7, 3, True)
         store(7, 3, 4)
         imp_sb = const.tile([P, P, NT], F32, name="imp_sb")
         nc.scalar.copy(out=imp_sb[:], in_=imp_t[:].rearrange("c t p -> c p t"))

from contextlib import ExitStack

import concourse.mybir as mybir
from concourse.masks import make_identity

F32 = mybir.dt.float32
BF16 = mybir.dt.bfloat16
U32 = mybir.dt.uint32
U8 = mybir.dt.uint8
FP8X4 = mybir.dt.float8_e4m3fn_x4
ACT = mybir.ActivationFunctionType
ALU = mybir.AluOpType

P = 128
NB = 8
S = 512
H = 512
I = 512
NT = 4
FLOPS = 3 * 2 * NB * S * H * I
HALF_S = S // 2

PINNED = True
GP_CAST = True
WARM_FIRST = 4
WARM_BETWEEN = 1
END_FROM = 29


def tile_qwen2mlp_nd_t_kernel(tc, hidden_state, w_gate, w_up, w_down, out_0, out_1):
    nc = tc.nc
    with ExitStack() as ctx:
        const = ctx.enter_context(tc.tile_pool(name="const", bufs=1))
        xin = ctx.enter_context(tc.tile_pool(name="xin", bufs=NB))
        work = ctx.enter_context(tc.tile_pool(name="work", bufs=2))
        psum = ctx.enter_context(tc.psum_pool(name="psum", bufs=2))
        if PINNED:
            ctx.enter_context(tc.manual_schedule())

        x_view = hidden_state.rearrange("b (p j) h -> b p j h", j=NT)
        o_view = out_0.rearrange("b (p j) n -> b p j n", j=NT)
        x_sb = {}
        w_sb = {}

        def load(raw, view, r0, r1):
            nc.sync.dma_start(out=raw[:].rearrange("p (r k) -> p r k", r=NT)[:, r0:r1, :], in_=view[:, r0:r1, :])

        for b in range(NB):
            x_raw = xin.tile([P, NT * H], BF16, name="x_raw")
            x_sb[b] = x_raw
        for key in ("g", "u", "d"):
            w_raw = const.tile([P, NT * H], BF16, name="w_raw_" + key)
            w_sb[key] = w_raw
        g_view = w_gate.rearrange("(p t) k -> p t k", t=NT)
        u_view = w_up.rearrange("(p t) k -> p t k", t=NT)
        load(x_sb[0], x_view[0], 0, 2)
        load(x_sb[0], x_view[0], 2, 4)
        load(w_sb["g"], g_view, 0, 2)
        load(w_sb["u"], u_view, 0, 2)
        load(w_sb["g"], g_view, 2, 4)
        load(w_sb["u"], u_view, 2, 4)
        load(x_sb[1], x_view[1], 0, 4)
        load(x_sb[2], x_view[2], 0, 4)
        load(w_sb["d"], w_down.rearrange("(r p) k -> p r k", p=P), 0, 4)
        for b in range(3, NB):
            load(x_sb[b], x_view[b], 0, 4)

        warm = const.tile([P, 2], F32, name="warm")
        nc.vector.memset(warm[:, 0:1], 1.0)
        nc.scalar.activation(out=warm[:, 1:2], in_=warm[:, 0:1], func=ACT.Silu)

        ident = const.tile([P, P], F32, name="ident")
        make_identity(nc, ident[:])
        imp_pad = const.tile([P, NT, P], F32, name="imp_pad")
        nc.gpsimd.memset(imp_pad[:], 0.0)
        ssum = const.tile([P, NB, NT], F32, name="ssum")
        row_sq = const.tile([P, NT], F32, name="row_sq")

        banks = {}
        grouped = {}
        codes = {}
        planes = {}

        def transposes(key, raw, pairs_apart, tag="xt", halves=(0, 1)):
            words = raw[:].bitcast(F32)
            if pairs_apart:
                view = words.rearrange("p (r q u) -> p r u q", r=NT, u=2)
            else:
                view = words.rearrange("p (r u q) -> p r u q", r=NT, u=2)
            for c in halves:
                bank = psum.tile([P, 2, 2 * P], F32, name=tag, tag=tag)
                for rr in range(2):
                    for u in range(2):
                        nc.tensor.transpose(bank[:, u, rr * P:(rr + 1) * P], view[:, 2 * c + rr, u, :], ident[:])
                banks[(key, c)] = bank

        def evacuate(key, c, on_scalar):
            if key not in grouped:
                grp = work.tile([P, 4 * S], BF16, name="grp", tag="grp", bufs=3, align_bytes=64)
                grouped[key] = grp
            dst = grouped[key][:].bitcast(F32).rearrange("p (s u) -> p s u", u=2)[:, c * 2 * P:(c + 1) * 2 * P, :]
            src = banks[(key, c)][:].rearrange("p u s -> p s u")
            if on_scalar:
                nc.scalar.copy(out=dst, in_=src)
            else:
                nc.vector.tensor_copy(out=dst, in_=src)

        def quantise(key, pool, bufs, tag, c0=0, c1=S):
            if key not in codes:
                cod = pool.tile([P, S], U32, name="cod_" + tag, tag="cod_" + tag, bufs=bufs, align_bytes=64)
                pla = pool.tile([P, S], U8, name="pla_" + tag, tag="pla_" + tag, bufs=bufs, align_bytes=64)
                codes[key] = cod
                planes[key] = pla
            nc.vector.quantize_mx(out=codes[key][:, c0:c1].bitcast(FP8X4), scales=planes[key][:, c0:c1],
                                  in_=grouped[key][:, 4 * c0:4 * c1])

        def ok(b):
            return 0 <= b < NB

        acc = {}
        sg = {}
        hf = {}

        def pass1(b, t, which):
            if not ok(b):
                return
            bank = psum.tile([P, S], F32, name="ps_" + which, tag="ps_" + which)
            cols = slice(t * P, (t + 1) * P)
            nc.tensor.matmul_mx(
                out=bank[:],
                lhsT=codes[which][:, cols].bitcast(FP8X4), lhsT_scale=planes[which][:, cols],
                rhs=codes[b][:].bitcast(FP8X4), rhs_scale=planes[b][:],
                start=True, stop=True)
            acc[(which, b, t)] = bank

        def silu(b, t):
            if not ok(b):
                return
            s_g = work.tile([P, S], F32, name="s_g", tag="s_g", bufs=4)
            nc.scalar.activation(out=s_g[:], in_=acc[("g", b, t)][:], func=ACT.Silu)
            sg[(b, t)] = s_g

        def mult(b, t):
            if not ok(b):
                return
            if t == 0:
                h_f = work.tile([P, NT, S], F32, name="h_f", tag="h_f", bufs=2)
                hf[b] = h_f
            nc.vector.tensor_tensor(out=hf[b][:, t, :], in0=sg[(b, t)][:], in1=acc[("u", b, t)][:], op=ALU.mult)

        def square(b, t):
            if not ok(b):
                return
            junk = work.tile([P, S], BF16, name="junk", tag="junk")
            nc.scalar.activation(out=junk[:], in_=hf[b][:, t, :], func=ACT.Square, accum_out=ssum[:, b, t:t + 1])

        def cast(b):
            if not ok(b):
                return
            grp = work.tile([P, 4 * S], BF16, name="hgrp", tag="hgrp", align_bytes=64)
            grouped[("h", b)] = grp
            dst = grp[:].rearrange("p (s t) -> p s t", t=NT)
            src = hf[b][:].rearrange("p t s -> p s t")
            if GP_CAST and b < NB - 1:
                nc.gpsimd.tensor_scalar(out=dst, in0=src, scalar1=1.0, scalar2=0.0, op0=ALU.mult, op1=ALU.add)
            else:
                nc.vector.tensor_copy(out=dst, in_=src)

        def cast_half(b, c):
            if c == 0:
                grp = work.tile([P, 4 * S], BF16, name="hgrp", tag="hgrp", align_bytes=64)
                grouped[("h", b)] = grp
            cols = slice(c * HALF_S, (c + 1) * HALF_S)
            dst = grouped[("h", b)][:].rearrange("p (s t) -> p s t", t=NT)[:, cols, :]
            src = hf[b][:].rearrange("p t s -> p s t")[:, cols, :]
            nc.vector.tensor_copy(out=dst, in_=src)

        def quant_h_half(b, c):
            quantise(("h", b), work, 2, "h", c * HALF_S, (c + 1) * HALF_S)

        def quant_h(b):
            if ok(b):
                quantise(("h", b), work, 2, "h")

        ob = {}

        def pass2(b, j, tag="ps_o"):
            if not ok(b):
                return
            bank = psum.tile([P, H], F32, name=tag, tag=tag)
            cols = slice(j * P, (j + 1) * P)
            nc.tensor.matmul_mx(
                out=bank[:],
                lhsT=codes[("h", b)][:, cols].bitcast(FP8X4), lhsT_scale=planes[("h", b)][:, cols],
                rhs=codes["d"][:].bitcast(FP8X4), rhs_scale=planes["d"][:],
                start=True, stop=True)
            acc[("o", b, j)] = bank

        def evac_o(b, j, on_scalar=False):
            if not ok(b):
                return
            if j == 0:
                o_sb = work.tile([P, NT, H], F32, name="o_sb", tag="o_sb", bufs=3)
                ob[b] = o_sb
            if on_scalar:
                nc.scalar.copy(out=ob[b][:, j, :], in_=acc[("o", b, j)][:])
            else:
                nc.vector.tensor_copy(out=ob[b][:, j, :], in_=acc[("o", b, j)][:])

        def store(b, j0, j1):
            if ok(b):
                nc.sync.dma_start(out=o_view[b][:, j0:j1, :], in_=ob[b][:, j0:j1, :])

        def prep_x_t(b):
            if ok(b):
                transposes(b, x_sb[b], False)

        wu3 = w_sb["u"][:].rearrange("p (t k) -> p t k", t=NT)

        def row_square(t):
            junk = work.tile([P, S], BF16, name="junk", tag="junk")
            nc.scalar.activation(out=junk[:], in_=wu3[:, t, :], func=ACT.Square, accum_out=row_sq[:, t:t + 1])

        def prep_x_q(b):
            if ok(b):
                quantise(b, work, 3, "x")

        zeros = const.tile([P, S], BF16, name="zeros")
        nc.vector.memset(zeros[:], 0.0)

        def keep_warm(count):
            for q in range(count):
                bank = psum.tile([P, S], F32, name="ps_u", tag="ps_u")
                nc.tensor.matmul(out=bank[:], lhsT=zeros[:, 0:P], rhs=zeros[:], start=True, stop=True)

        HALF = S // 2
        keep_warm(WARM_FIRST)
        transposes(0, x_sb[0], False)
        keep_warm(WARM_BETWEEN)
        transposes("g", w_sb["g"], False, "ps_o", (0,))
        transposes("u", w_sb["u"], False, "ps_o", (0,))
        keep_warm(WARM_BETWEEN)
        evacuate(0, 0, True)
        evacuate(0, 1, False)
        quantise(0, work, 3, "x")
        transposes("g", w_sb["g"], False, "xt", (1,))
        transposes("u", w_sb["u"], False, "xt", (1,))
        evacuate("g", 0, True)
        quantise("g", const, 1, "wg", 0, HALF)
        pass1(0, 0, "g")
        pass1(0, 1, "g")
        evacuate("u", 0, True)
        quantise("u", const, 1, "wu", 0, HALF)
        pass1(0, 0, "u")
        pass1(0, 1, "u")
        evacuate("u", 1, False)
        evacuate("g", 1, True)
        quantise("g", const, 1, "wg", HALF, S)
        quantise("u", const, 1, "wu", HALF, S)
        transposes(1, x_sb[1], False, "ps_o")

        silu(0, 0)
        pass1(0, 2, "g")
        row_square(0)
        mult(0, 0)
        pass1(0, 2, "u")
        transposes(2, x_sb[2], False)
        silu(0, 1)
        pass1(0, 3, "g")
        evacuate(1, 0, True)
        mult(0, 1)
        pass1(0, 3, "u")
        evacuate(1, 1, False)
        prep_x_q(1)
        transposes("d", w_sb["d"], True, "ps_o")
        silu(0, 2)
        pass1(1, 0, "g")
        square(0, 0)
        evacuate(2, 1, True)
        mult(0, 2)
        pass1(1, 0, "u")
        evacuate(2, 0, False)
        prep_x_t(3)
        prep_x_q(2)
        silu(0, 3)
        pass1(1, 1, "g")
        square(0, 1)
        mult(0, 3)
        cast(0)
        pass1(1, 1, "u")

        L = NB - 1
        LAST = NT * NB - 1
        for n in range(NT, END_FROM):
            i, t = divmod(n, NT)
            silu(i, t)
            pass1((n + 2) // NT, (n + 2) % NT, "g")
            if t == 3:
                pass2(i - 1, 0)
                pass2(i - 1, 1)
            if n == LAST:
                pass2(L - 1, 2, "ps_g")
                pass2(L - 1, 3, "ps_g")
                nc.scalar.activation(out=warm[:, 1:2], in_=warm[:, 0:1], func=ACT.Sqrt)
            square((n - 2) // NT, (n - 2) % NT)
            if n == LAST - NT:
                row_square(1)
            if i == 1:
                if t == 1:
                    evacuate(3, t, True)
            elif t == 0:
                if ok(i + 2):
                    evacuate(i + 2, 1, True)
                elif i == NB - 2:
                    row_square(3)
            if t == 3:
                if ok(i + 3):
                    evacuate(i + 3, 0, True)
                elif i == NB - 3:
                    row_square(2)
            mult(i, t)
            if t == 3:
                cast(i)
            pass1((n + 2) // NT, (n + 2) % NT, "u")
            if i == 1 and t < 2:
                evacuate("d", t, False)
                if t == 0:
                    evacuate(3, t, False)
            elif 7 <= n < LAST:
                b, j = divmod(n - 7, NT)
                evac_o(b, j)
                if j % 2 == 1:
                    store(b, j - 1, j + 1)
                if j < 2:
                    pass2(b, j + 2)
            if t == 1:
                prep_x_t(i + 3)
            if t == 2:
                if i == 1:
                    quantise("d", const, 1, "wd")
                quant_h(i - 1)
                prep_x_q(i + 2)

        silu(7, 1)
        pass1(7, 3, "g")
        square(6, 3)
        mult(7, 1)
        pass1(7, 3, "u")
        evac_o(5, 2)
        quant_h(6)
        silu(7, 2)
        pass2(6, 0, "xt")
        pass2(6, 1, "xt")
        square(7, 0)
        mult(7, 2)
        evac_o(5, 3)
        store(5, 2, 4)
        silu(7, 3)
        pass2(6, 2, "ps_g")
        pass2(6, 3, "ps_g")
        nc.scalar.activation(out=warm[:, 1:2], in_=warm[:, 0:1], func=ACT.Sqrt)
        evac_o(6, 0, True)
        evac_o(6, 1, True)
        store(6, 0, 2)
        mult(7, 3)
        cast_half(7, 0)
        quant_h_half(7, 0)
        pass2(7, 0, "ps_u")
        pass2(7, 1, "ps_u")
        cast_half(7, 1)
        quant_h_half(7, 1)
        pass2(7, 2, "ps_o")
        pass2(7, 3, "ps_o")
        evac_o(6, 2, True)
        evac_o(6, 3, True)
        store(6, 2, 4)
        imp_t = psum.tile([P, NT, P], F32, name="imp_t", tag="xt")
        for t in range(NT):
            if t > 0:
                square(7, t)
            nc.scalar.activation(out=imp_pad[:, t, 0:NB], in_=ssum[:, :, t], func=ACT.Sqrt, scale=row_sq[:, t:t + 1])
            nc.tensor.transpose(imp_t[:, t, :], imp_pad[:, t, :], ident[:])
        evac_o(7, 0)
        store(7, 0, 1)
        evac_o(7, 1)
        store(7, 1, 2)
        evac_o(7, 2)
        store(7, 2, 3)
        evac_o(7, 3, True)
        store(7, 3, 4)
        imp_sb = const.tile([P, P, NT], F32, name="imp_sb")
        nc.scalar.copy(out=imp_sb[:], in_=imp_t[:].rearrange("c t p -> c p t"))
        nc.sync.dma_start(out=out_1, in_=imp_sb[0:NB].rearrange("c p t -> c (p t)"))
